import numpy as np
import ml_dtypes


def mxq(x, axis, fmt="e4m3"):
    dtype, down = {"e4m3": (ml_dtypes.float8_e4m3fn, 7), "e5m2": (ml_dtypes.float8_e5m2, 14)}[fmt]
    v = np.moveaxis(np.asarray(x, np.float32).astype(ml_dtypes.bfloat16).astype(np.float64), axis, -1)
    blocks = v.reshape(v.shape[:-1] + (-1, 32))
    amax = np.abs(blocks).max(-1, keepdims=True)
    byte = np.maximum(np.where(amax > 0, np.frexp(amax)[1] - 1 + 127, 0) - down, 1)
    scale = np.exp2(byte - 127.0)
    codes = (blocks / scale).astype(np.float32).astype(dtype).astype(np.float64)
    return np.moveaxis((codes * scale).reshape(v.shape), -1, axis)


WIDE = False


def mx_kscale(k):
    if not WIDE:
        return np.ones(k)
    levels = np.array([10, -10, 5, -5, 0])
    a = np.random.permutation(np.resize(levels, k // 512 * 4)).reshape(k // 512, 4)
    idx = np.arange(k)
    return np.exp2(a[idx // 512, idx % 128 // 32])


BF16 = ml_dtypes.bfloat16


def bf(x):
    return np.asarray(x, np.float32).astype(BF16)


def f64(x):
    return np.asarray(x).astype(np.float64)


B, C, H, W, K = 2, 512, 16, 16, 128
N = H * W
XS = 1.6 / C ** 0.25
CS = 0.4 / C ** 0.25


def setup_inputs():
    s = mx_kscale(C)
    return {'x': bf(np.random.standard_normal((B, C, H, W)) * s[None, :, None, None]),
            'conv_w': bf(np.random.standard_normal((C, C)) * XS / np.sqrt(C) / s[None, :]),
            'conv_b': bf(np.random.standard_normal(C) * 0.4 * XS),
            'codebook': bf(np.random.standard_normal((K, C)) * CS),
            'log_smooth': bf(np.random.standard_normal(K) * 0.25 / np.sqrt(C))}


def reference(x, conv_w, conv_b, codebook, log_smooth):
    x, conv_w, conv_b, codebook, log_smooth = f64(x), f64(conv_w), f64(conv_b), f64(codebook), f64(log_smooth)
    b, c, h, w = x.shape
    xp = (mxq(conv_w, 1, 'e4m3') @ mxq(x.reshape(b, c, h * w), 1, 'e4m3')) + conv_b[None, :, None]
    xp = xp.transpose(0, 2, 1)
    smooth = np.exp(log_smooth)
    x2 = np.sum(xp * xp, axis=-1)
    c2 = np.sum(codebook * codebook, axis=-1)
    xc = mxq(xp, 2, 'e4m3') @ mxq(codebook, 1, 'e4m3').T
    dist_sq = x2[:, :, None] - 2.0 * xc + c2[None, None, :]
    z = -smooth[None, None, :] * dist_sq
    ez = np.exp(z - z.max(axis=2, keepdims=True))
    assign = ez / ez.sum(axis=2, keepdims=True)
    return xp, assign

@@ -1,0 +1,317 @@
+from contextlib import ExitStack
+
+import concourse.mybir as mybir
+from concourse.masks import make_identity
+
+F32 = mybir.dt.float32
+BF16 = mybir.dt.bfloat16
+U32 = mybir.dt.uint32
+U8 = mybir.dt.uint8
+FP8X4 = mybir.dt.float8_e4m3fn_x4
+ALU = mybir.AluOpType
+ACT = mybir.ActivationFunctionType
+AXIS = mybir.AxisListType
+
+P = 128
+PACK = 4
+IMAGES = 2
+CHANNELS = 512
+PIXELS = 256
+CODEWORDS = 128
+BLOCKS_PER_IMAGE = PIXELS // P
+PIXEL_BLOCKS = IMAGES * BLOCKS_PER_IMAGE
+CHANNEL_BLOCKS = CHANNELS // P
+
+FLOPS = 2 * IMAGES * PIXELS * CHANNELS * (CHANNELS + CODEWORDS)
+
+
+def tile_lvc_pa_s_kernel(tc, x, conv_w, conv_b, codebook, log_smooth, out_0, out_1):
+    nc = tc.nc
+    with ExitStack() as ctx:
+        keep = ctx.enter_context(tc.tile_pool(name="keep", bufs=1))
+        psum_turned = ctx.enter_context(tc.psum_pool(name="psum_turned", bufs=3))
+        psum_conv = ctx.enter_context(tc.psum_pool(name="psum_conv", bufs=PIXEL_BLOCKS))
+        psum_xc = ctx.enter_context(tc.psum_pool(name="psum_xc", bufs=1))
+        ctx.enter_context(tc.manual_schedule())
+
+        vector_row = keep.tile([1, CHANNELS + CODEWORDS], BF16)
+        vectors = keep.tile([P, CHANNELS + CODEWORDS], BF16)
+        ones = keep.tile([P, P], BF16)
+        table_warmer = keep.tile([P, 1], F32)
+        identity_f32 = keep.tile([P, P], F32)
+        identity_bf16 = keep.tile([P, P], BF16)
+        bias_rows = keep.tile([P, CHANNELS], F32)
+        smooth_rows = keep.tile([P, CODEWORDS], F32)
+        c2_column = keep.tile([P, 1], F32)
+        c2_rows = keep.tile([P, CODEWORDS], F32)
+
+        w_raw = keep.tile([P, CHANNEL_BLOCKS, CHANNELS], BF16)
+        w_grouped = keep.tile([P, CHANNELS * PACK], BF16, align_bytes=64)
+        w_codes = keep.tile([P, CHANNELS], U32, align_bytes=64)
+        w_scales = keep.tile([P, CHANNELS], U8, align_bytes=64)
+        x_raw = keep.tile([P, IMAGES, PACK, PIXELS], BF16)
+        x_grouped = keep.tile([P, IMAGES, PIXELS, PACK], BF16, align_bytes=64)
+        x_codes = keep.tile([P, IMAGES * PIXELS], U32, align_bytes=64)
+        x_scales = keep.tile([P, IMAGES * PIXELS], U8, align_bytes=64)
+        codebook_raw = keep.tile([P, CHANNELS], BF16)
+        codebook_squares = keep.tile([P, CHANNELS], BF16)
+        codebook_grouped = keep.tile([P, CODEWORDS, PACK], BF16, align_bytes=64)
+        codebook_codes = keep.tile([P, CODEWORDS], U32, align_bytes=64)
+        codebook_scales = keep.tile([P, CODEWORDS], U8, align_bytes=64)
+
+        xp = keep.tile([P, PIXEL_BLOCKS, CHANNELS], F32)
+        xp_squares = keep.tile([P, PIXEL_BLOCKS, CHANNELS], BF16)
+        x2 = keep.tile([P, PIXEL_BLOCKS], F32)
+        xp_grouped = keep.tile([P, PIXEL_BLOCKS, P, PACK], BF16, align_bytes=64)
+        xp_codes = keep.tile([P, PIXEL_BLOCKS, P], U32, align_bytes=64)
+        xp_scales = keep.tile([P, PIXEL_BLOCKS, P], U8, align_bytes=64)
+        xc = psum_xc.tile([P, PIXEL_BLOCKS, CODEWORDS], F32)
+        cross = keep.tile([P, PIXEL_BLOCKS, CODEWORDS], F32)
+        scaled = keep.tile([P, PIXEL_BLOCKS, CODEWORDS], F32)
+        nearest = keep.tile([P, PIXEL_BLOCKS], F32)
+        weights = keep.tile([P, PIXEL_BLOCKS, CODEWORDS], F32)
+        weight_sums = keep.tile([P, PIXEL_BLOCKS], F32)
+        inverse_sums = keep.tile([P, PIXEL_BLOCKS], F32)
+        assign = keep.tile([P, PIXEL_BLOCKS, CODEWORDS], F32)
+        out_0_view = out_0.rearrange("b (s p) c -> p (b s) c", p=P)
+        out_1_view = out_1.rearrange("b (s p) k -> p (b s) k", p=P)
+        conv = [psum_conv.tile([P, CHANNELS], F32, name="conv", tag="conv") for j in range(PIXEL_BLOCKS)]
+
+        def load_w(half):
+            obs = slice(2 * half, 2 * half + 2)
+            nc.sync.dma_start(out=w_raw[:, obs, :], in_=conv_w.rearrange("(ob p) c -> p ob c", p=P)[:, obs, :])
+
+        def load_x(b):
+            nc.sync.dma_start(
+                out=x_raw[:, b].rearrange("q (u e) n -> q u (e n)", u=2),
+                in_=x[b].rearrange("(u q e) h w -> q u (e h w)", u=2, e=2),
+            )
+
+        def turn_w(half):
+            w_turned = psum_turned.tile([P, 2, 2 * P], F32, tag="turned")
+            for side in range(2):
+                for u in range(2):
+                    nc.tensor.transpose(
+                        out=w_turned[:, u, side * P : (side + 1) * P],
+                        in_=w_raw[:, 2 * half + side, 2 * P * u : 2 * P * (u + 1)].bitcast(F32),
+                        identity=identity_f32[:],
+                    )
+            values = slice(half * 2 * P * PACK, (half + 1) * 2 * P * PACK)
+            nc.scalar.copy(
+                out=w_grouped[:, values].bitcast(F32).rearrange("p (o u) -> p o u", u=2),
+                in_=w_turned[:].rearrange("p u o -> p o u"),
+            )
+
+        def quantise_w(half):
+            values = slice(half * 2 * P * PACK, (half + 1) * 2 * P * PACK)
+            words = slice(half * 2 * P, (half + 1) * 2 * P)
+            nc.vector.quantize_mx(
+                out=w_codes[:, words].bitcast(FP8X4), scales=w_scales[:, words], in_=w_grouped[:, values]
+            )
+
+        def regroup_x(b):
+            nc.vector.tensor_copy(
+                out=x_grouped[:, b].rearrange("q (c i) t -> q c t i", i=4),
+                in_=x_raw[:, b].rearrange("q t (c i) -> q c t i", i=4),
+            )
+
+        def quantise_x(b):
+            words = slice(b * PIXELS, (b + 1) * PIXELS)
+            nc.vector.quantize_mx(
+                out=x_codes[:, words].bitcast(FP8X4),
+                scales=x_scales[:, words],
+                in_=x_grouped[:, b].rearrange("q n t -> q (n t)"),
+            )
+
+        def convolve(j):
+            pixels = slice(j * P, (j + 1) * P)
+            nc.tensor.matmul_mx(
+                out=conv[j][:],
+                lhsT=x_codes[:, pixels].bitcast(FP8X4),
+                lhsT_scale=x_scales[:, pixels],
+                rhs=w_codes[:].bitcast(FP8X4),
+                rhs_scale=w_scales[:],
+                start=True,
+                stop=True,
+            )
+
+        def add_bias(j):
+            nc.vector.tensor_tensor(out=xp[:, j, :], in0=conv[j][:], in1=bias_rows[:], op=ALU.add)
+            nc.sync.dma_start(out=out_0_view[:, j, :], in_=xp[:, j, :])
+
+        def sum_squares(j):
+            nc.scalar.activation(
+                out=xp_squares[:, j, :], in_=xp[:, j, :], func=ACT.Square, accum_out=x2[:, j : j + 1]
+            )
+
+        def turn_xp(j):
+            xp_turned = psum_turned.tile([P, PACK, P], F32, tag="turned")
+            for t in range(PACK):
+                nc.tensor.transpose(
+                    out=xp_turned[:, t, :], in_=xp[:, j, t * P : (t + 1) * P], identity=identity_f32[:]
+                )
+            return xp_turned
+
+        def regroup_xp(j, xp_turned):
+            nc.scalar.copy(out=xp_grouped[:, j], in_=xp_turned[:].rearrange("p t n -> p n t"))
+
+        def quantise_xp(j):
+            nc.vector.quantize_mx(
+                out=xp_codes[:, j, :].bitcast(FP8X4),
+                scales=xp_scales[:, j, :],
+                in_=xp_grouped[:, j].rearrange("p n t -> p (n t)"),
+            )
+
+        def multiply_codebook(j):
+            nc.tensor.matmul_mx(
+                out=xc[:, j, :],
+                lhsT=xp_codes[:, j, :].bitcast(FP8X4),
+                lhsT_scale=xp_scales[:, j, :],
+                rhs=codebook_codes[:].bitcast(FP8X4),
+                rhs_scale=codebook_scales[:],
+                start=True,
+                stop=True,
+            )
+
+        def blocks_of(b):
+            return slice(b * BLOCKS_PER_IMAGE, (b + 1) * BLOCKS_PER_IMAGE)
+
+        def cross_terms(b):
+            nc.vector.scalar_tensor_tensor(
+                out=cross[:, blocks_of(b), :],
+                in0=xc[:, blocks_of(b), :],
+                scalar=-2.0,
+                in1=c2_rows[:].unsqueeze(1).to_broadcast([P, BLOCKS_PER_IMAGE, CODEWORDS]),
+                op0=ALU.mult,
+                op1=ALU.add,
+            )
+
+        def scale_distances(j):
+            nc.vector.scalar_tensor_tensor(
+                out=scaled[:, j, :],
+                in0=cross[:, j, :],
+                scalar=x2[:, j : j + 1],
+                in1=smooth_rows[:],
+                op0=ALU.add,
+                op1=ALU.mult,
+            )
+
+        def find_nearest(j):
+            nc.vector.tensor_reduce(out=nearest[:, j : j + 1], in_=scaled[:, j, :], axis=AXIS.X, op=ALU.min)
+
+        def exponentials(j):
+            nc.scalar.activation(
+                out=weights[:, j, :],
+                in_=scaled[:, j, :],
+                func=ACT.Exp,
+                scale=-1.0,
+                bias=nearest[:, j : j + 1],
+                accum_out=weight_sums[:, j : j + 1],
+            )
+
+        def invert_sum(j):
+            nc.vector.reciprocal(out=inverse_sums[:, j : j + 1], in_=weight_sums[:, j : j + 1])
+
+        def normalise(j):
+            nc.vector.tensor_scalar_mul(out=assign[:, j, :], in0=weights[:, j, :], scalar1=inverse_sums[:, j : j + 1])
+            nc.sync.dma_start(out=out_1_view[:, j, :], in_=assign[:, j, :])
+
+        nc.sync.dma_start(out=vector_row[:, 0:CHANNELS], in_=conv_b.unsqueeze(0))
+        nc.sync.dma_start(out=vector_row[:, CHANNELS:], in_=log_smooth.unsqueeze(0))
+        nc.vector.memset(ones[:], 1.0)
+        nc.vector.memset(vectors[:], 0.0)
+        load_w(0)
+        load_w(1)
+        load_x(0)
+        load_x(1)
+        nc.sync.dma_start(out=codebook_raw[:], in_=codebook)
+        make_identity(nc, identity_f32[:])
+        make_identity(nc, identity_bf16[:])
+        nc.scalar.activation(out=table_warmer[:], in_=ones[:, 0:1], func=ACT.Exp)
+
+        nc.vector.tensor_copy(out=vectors[0:1, :], in_=vector_row[:])
+        bias_spread = psum_turned.tile([P, CHANNELS], F32, tag="turned")
+        nc.tensor.matmul(out=bias_spread[:], lhsT=ones[:], rhs=vectors[:, 0:CHANNELS], start=True, stop=True)
+        nc.vector.tensor_copy(out=bias_rows[:], in_=bias_spread[:])
+        log_smooth_spread = psum_turned.tile([P, CODEWORDS], F32, tag="turned")
+        nc.tensor.matmul(out=log_smooth_spread[:], lhsT=ones[:], rhs=vectors[:, CHANNELS:], start=True, stop=True)
+        nc.scalar.activation(out=smooth_rows[:], in_=log_smooth_spread[:], func=ACT.Exp)
+
+        turn_w(0)
+        turn_w(1)
+        regroup_x(0)
+        quantise_w(0)
+        quantise_x(0)
+        quantise_w(1)
+        regroup_x(1)
+
+        nc.scalar.activation(
+            out=codebook_squares[:], in_=codebook_raw[:], func=ACT.Square, accum_out=c2_column[:]
+        )
+        codebook_turned = psum_turned.tile([P, PACK, CODEWORDS], BF16, tag="turned")
+        for t in range(PACK):
+            nc.tensor.transpose(
+                out=codebook_turned[:, t, :], in_=codebook_raw[:, t * P : (t + 1) * P], identity=identity_bf16[:]
+            )
+        nc.scalar.copy(out=codebook_grouped[:], in_=codebook_turned[:].rearrange("p t k -> p k t"))
+
+        convolve(0)
+        convolve(1)
+        add_bias(0)
+        sum_squares(0)
+        xp_turned_0 = turn_xp(0)
+        regroup_xp(0, xp_turned_0)
+        quantise_x(1)
+        convolve(2)
+        convolve(3)
+        add_bias(1)
+        sum_squares(1)
+        nc.vector.quantize_mx(
+            out=codebook_codes[:].bitcast(FP8X4),
+            scales=codebook_scales[:],
+            in_=codebook_grouped[:].rearrange("p k t -> p (k t)"),
+        )
+        c2_turned = psum_turned.tile([P, CODEWORDS], F32, tag="turned")
+        nc.tensor.transpose(out=c2_turned[:], in_=c2_column[:, 0:1].to_broadcast([P, P]), identity=identity_f32[:])
+        xp_turned_1 = turn_xp(1)
+        regroup_xp(1, xp_turned_1)
+        add_bias(2)
+        nc.vector.tensor_copy(out=c2_rows[:], in_=c2_turned[:])
+        xp_turned_2 = turn_xp(2)
+        regroup_xp(2, xp_turned_2)
+        add_bias(3)
+        xp_turned_3 = turn_xp(3)
+        regroup_xp(3, xp_turned_3)
+        sum_squares(2)
+        sum_squares(3)
+
+        quantise_xp(0)
+        quantise_xp(1)
+        multiply_codebook(0)
+        multiply_codebook(1)
+        quantise_xp(2)
+        multiply_codebook(2)
+        cross_terms(0)
+        quantise_xp(3)
+        multiply_codebook(3)
+        scale_distances(0)
+        scale_distances(1)
+        find_nearest(0)
+        find_nearest(1)
+        exponentials(0)
+        exponentials(1)
+        cross_terms(1)
+        scale_distances(2)
+        scale_distances(3)
+        find_nearest(2)
+        find_nearest(3)
+        exponentials(2)
+        exponentials(3)
+        invert_sum(0)
+        invert_sum(1)
+        normalise(0)
+        normalise(1)
+        invert_sum(2)
+        normalise(2)
+        invert_sum(3)
+        normalise(3)

@@ -41,6 +41,7 @@ def tile_lvc_pa_s_kernel(tc, x, conv_w, conv_b, codebook, log_smooth, out_0, out
         identity_f32 = keep.tile([P, P], F32)
         identity_bf16 = keep.tile([P, P], BF16)
         bias_rows = keep.tile([P, CHANNELS], F32)
+        bias_columns = keep.tile([P, PACK], F32)
         smooth_rows = keep.tile([P, CODEWORDS], F32)
         c2_column = keep.tile([P, 1], F32)
         c2_rows = keep.tile([P, CODEWORDS], F32)
@@ -109,10 +110,10 @@ def tile_lvc_pa_s_kernel(tc, x, conv_w, conv_b, codebook, log_smooth, out_0, out
                 out=w_codes[:, words].bitcast(FP8X4), scales=w_scales[:, words], in_=w_grouped[:, values]
             )
 
-        def regroup_x(b):
-            nc.vector.tensor_copy(
-                out=x_grouped[:, b].rearrange("q (c i) t -> q c t i", i=4),
-                in_=x_raw[:, b].rearrange("q t (c i) -> q c t i", i=4),
+        def regroup_x(copy, b, pixels):
+            copy(
+                out=x_grouped[:, b, pixels, :].rearrange("q (c i) t -> q c t i", i=4),
+                in_=x_raw[:, b, :, pixels].rearrange("q t (c i) -> q c t i", i=4),
             )
 
         def quantise_x(b):
@@ -154,6 +155,30 @@ def tile_lvc_pa_s_kernel(tc, x, conv_w, conv_b, codebook, log_smooth, out_0, out
 
         def regroup_xp(j, xp_turned):
             nc.scalar.copy(out=xp_grouped[:, j], in_=xp_turned[:].rearrange("p t n -> p n t"))
+
+        def convolve_turned(j):
+            pixels = slice(j * P, (j + 1) * P)
+            conv_turned = psum_turned.tile([P, PACK, P], F32, tag="turned")
+            for t in range(PACK):
+                channels = slice(t * P, (t + 1) * P)
+                nc.tensor.matmul_mx(
+                    out=conv_turned[:, t, :],
+                    lhsT=w_codes[:, channels].bitcast(FP8X4),
+                    lhsT_scale=w_scales[:, channels],
+                    rhs=x_codes[:, pixels].bitcast(FP8X4),
+                    rhs_scale=x_scales[:, pixels],
+                    start=True,
+                    stop=True,
+                )
+            return conv_turned
+
+        def add_bias_grouped(j, conv_turned):
+            nc.vector.tensor_tensor(
+                out=xp_grouped[:, j],
+                in0=conv_turned[:].rearrange("p t n -> p n t"),
+                in1=bias_columns[:].unsqueeze(1).to_broadcast([P, P, PACK]),
+                op=ALU.add,
+            )
 
         def quantise_xp(j):
             nc.vector.quantize_mx(
@@ -221,8 +246,8 @@ def tile_lvc_pa_s_kernel(tc, x, conv_w, conv_b, codebook, log_smooth, out_0, out
         nc.vector.memset(ones[:], 1.0)
         nc.vector.memset(vectors[:], 0.0)
         load_w(0)
-        load_w(1)
         load_x(0)
+        load_w(1)
         load_x(1)
         nc.sync.dma_start(out=codebook_raw[:], in_=codebook)
         make_identity(nc, identity_f32[:])
@@ -230,20 +255,31 @@ def tile_lvc_pa_s_kernel(tc, x, conv_w, conv_b, codebook, log_smooth, out_0, out
         nc.scalar.activation(out=table_warmer[:], in_=ones[:, 0:1], func=ACT.Exp)
 
         nc.vector.tensor_copy(out=vectors[0:1, :], in_=vector_row[:])
+        turn_w(0)
         bias_spread = psum_turned.tile([P, CHANNELS], F32, tag="turned")
         nc.tensor.matmul(out=bias_spread[:], lhsT=ones[:], rhs=vectors[:, 0:CHANNELS], start=True, stop=True)
+        small = psum_turned.tile([P, CODEWORDS + PACK], F32, tag="turned")
+        log_smooth_spread = small[:, 0:CODEWORDS]
+        nc.tensor.matmul(out=log_smooth_spread, lhsT=ones[:], rhs=vectors[:, CHANNELS:], start=True, stop=True)
+        for t in range(PACK):
+            nc.tensor.matmul(
+                out=small[:, CODEWORDS + t : CODEWORDS + t + 1],
+                lhsT=vectors[:, t * P : (t + 1) * P],
+                rhs=ones[:, 0:1],
+                start=True,
+                stop=True,
+            )
+        nc.scalar.activation(out=smooth_rows[:], in_=log_smooth_spread, func=ACT.Exp)
+        nc.scalar.copy(out=bias_columns[:], in_=small[:, CODEWORDS:])
+        regroup_x(nc.vector.tensor_copy, 0, slice(0, PIXELS))
         nc.vector.tensor_copy(out=bias_rows[:], in_=bias_spread[:])
-        log_smooth_spread = psum_turned.tile([P, CODEWORDS], F32, tag="turned")
-        nc.tensor.matmul(out=log_smooth_spread[:], lhsT=ones[:], rhs=vectors[:, CHANNELS:], start=True, stop=True)
-        nc.scalar.activation(out=smooth_rows[:], in_=log_smooth_spread[:], func=ACT.Exp)
-
-        turn_w(0)
-        turn_w(1)
-        regroup_x(0)
         quantise_w(0)
         quantise_x(0)
+        turn_w(1)
+        regroup_x(nc.scalar.copy, 1, slice(0, P))
+        regroup_x(nc.vector.tensor_copy, 1, slice(P, PIXELS))
         quantise_w(1)
-        regroup_x(1)
+        quantise_x(1)
 
         nc.scalar.activation(
             out=codebook_squares[:], in_=codebook_raw[:], func=ACT.Square, accum_out=c2_column[:]
@@ -257,50 +293,49 @@ def tile_lvc_pa_s_kernel(tc, x, conv_w, conv_b, codebook, log_smooth, out_0, out
 
         convolve(0)
         convolve(1)
+        convolve(2)
+        conv_turned_3 = convolve_turned(3)
+        convolve(3)
         add_bias(0)
         sum_squares(0)
         xp_turned_0 = turn_xp(0)
         regroup_xp(0, xp_turned_0)
-        quantise_x(1)
-        convolve(2)
-        convolve(3)
         add_bias(1)
-        sum_squares(1)
+        xp_turned_1 = turn_xp(1)
+        regroup_xp(1, xp_turned_1)
+        add_bias(2)
+        add_bias_grouped(3, conv_turned_3)
         nc.vector.quantize_mx(
             out=codebook_codes[:].bitcast(FP8X4),
             scales=codebook_scales[:],
             in_=codebook_grouped[:].rearrange("p k t -> p (k t)"),
         )
+        xp_turned_2 = turn_xp(2)
         c2_turned = psum_turned.tile([P, CODEWORDS], F32, tag="turned")
         nc.tensor.transpose(out=c2_turned[:], in_=c2_column[:, 0:1].to_broadcast([P, P]), identity=identity_f32[:])
-        xp_turned_1 = turn_xp(1)
-        regroup_xp(1, xp_turned_1)
-        add_bias(2)
-        nc.vector.tensor_copy(out=c2_rows[:], in_=c2_turned[:])
-        xp_turned_2 = turn_xp(2)
         regroup_xp(2, xp_turned_2)
-        add_bias(3)
-        xp_turned_3 = turn_xp(3)
-        regroup_xp(3, xp_turned_3)
-        sum_squares(2)
-        sum_squares(3)
-
+        nc.scalar.copy(out=c2_rows[:], in_=c2_turned[:])
         quantise_xp(0)
-        quantise_xp(1)
+        quantise_xp(3)
         multiply_codebook(0)
+        multiply_codebook(3)
+        add_bias(3)
+        quantise_xp(1)
         multiply_codebook(1)
         quantise_xp(2)
         multiply_codebook(2)
+        sum_squares(1)
+        sum_squares(2)
+        sum_squares(3)
+
         cross_terms(0)
-        quantise_xp(3)
-        multiply_codebook(3)
+        cross_terms(1)
         scale_distances(0)
         scale_distances(1)
         find_nearest(0)
         find_nearest(1)
         exponentials(0)
         exponentials(1)
-        cross_terms(1)
         scale_distances(2)
         scale_distances(3)
         find_nearest(2)
@@ -312,6 +347,6 @@ def tile_lvc_pa_s_kernel(tc, x, conv_w, conv_b, codebook, log_smooth, out_0, out
         normalise(0)
         normalise(1)
         invert_sum(2)
-        normalise(2)
         invert_sum(3)
+        normalise(2)
         normalise(3)

@@ -246,8 +246,8 @@ def tile_lvc_pa_s_kernel(tc, x, conv_w, conv_b, codebook, log_smooth, out_0, out
         nc.vector.memset(ones[:], 1.0)
         nc.vector.memset(vectors[:], 0.0)
         load_w(0)
-        load_x(0)
         load_w(1)
+        load_x(0)
         load_x(1)
         nc.sync.dma_start(out=codebook_raw[:], in_=codebook)
         make_identity(nc, identity_f32[:])

@@ -34,7 +34,6 @@ def tile_lvc_pa_s_kernel(tc, x, conv_w, conv_b, codebook, log_smooth, out_0, out
         psum_xc = ctx.enter_context(tc.psum_pool(name="psum_xc", bufs=1))
         ctx.enter_context(tc.manual_schedule())
 
-        vector_row = keep.tile([1, CHANNELS + CODEWORDS], BF16)
         vectors = keep.tile([P, CHANNELS + CODEWORDS], BF16)
         ones = keep.tile([P, P], BF16)
         table_warmer = keep.tile([P, 1], F32)
@@ -76,7 +75,6 @@ def tile_lvc_pa_s_kernel(tc, x, conv_w, conv_b, codebook, log_smooth, out_0, out
         assign = keep.tile([P, PIXEL_BLOCKS, CODEWORDS], F32)
         out_0_view = out_0.rearrange("b (s p) c -> p (b s) c", p=P)
         out_1_view = out_1.rearrange("b (s p) k -> p (b s) k", p=P)
-        conv = [psum_conv.tile([P, CHANNELS], F32, name="conv", tag="conv") for j in range(PIXEL_BLOCKS)]
 
         def load_w(half):
             obs = slice(2 * half, 2 * half + 2)
@@ -88,24 +86,26 @@ def tile_lvc_pa_s_kernel(tc, x, conv_w, conv_b, codebook, log_smooth, out_0, out
                 in_=x[b].rearrange("(u q e) h w -> q u (e h w)", u=2, e=2),
             )
 
-        def turn_w(half):
-            w_turned = psum_turned.tile([P, 2, 2 * P], F32, tag="turned")
-            for side in range(2):
-                for u in range(2):
-                    nc.tensor.transpose(
-                        out=w_turned[:, u, side * P : (side + 1) * P],
-                        in_=w_raw[:, 2 * half + side, 2 * P * u : 2 * P * (u + 1)].bitcast(F32),
-                        identity=identity_f32[:],
-                    )
-            values = slice(half * 2 * P * PACK, (half + 1) * 2 * P * PACK)
-            nc.scalar.copy(
+        def turn_w(ob):
+            w_turned = psum_conv.tile([P, 2, P], F32, name="w_turned", tag="conv")
+            for u in range(2):
+                nc.tensor.transpose(
+                    out=w_turned[:, u, :],
+                    in_=w_raw[:, ob, 2 * P * u : 2 * P * (u + 1)].bitcast(F32),
+                    identity=identity_f32[:],
+                )
+            return w_turned
+
+        def regroup_w(copy, ob, w_turned):
+            values = slice(ob * P * PACK, (ob + 1) * P * PACK)
+            copy(
                 out=w_grouped[:, values].bitcast(F32).rearrange("p (o u) -> p o u", u=2),
                 in_=w_turned[:].rearrange("p u o -> p o u"),
             )
 
-        def quantise_w(half):
-            values = slice(half * 2 * P * PACK, (half + 1) * 2 * P * PACK)
-            words = slice(half * 2 * P, (half + 1) * 2 * P)
+        def quantise_w(first, count):
+            values = slice(first * P * PACK, (first + count) * P * PACK)
+            words = slice(first * P, (first + count) * P)
             nc.vector.quantize_mx(
                 out=w_codes[:, words].bitcast(FP8X4), scales=w_scales[:, words], in_=w_grouped[:, values]
             )
@@ -126,8 +126,9 @@ def tile_lvc_pa_s_kernel(tc, x, conv_w, conv_b, codebook, log_smooth, out_0, out
 
         def convolve(j):
             pixels = slice(j * P, (j + 1) * P)
+            conv = psum_conv.tile([P, CHANNELS], F32, name="conv", tag="conv")
             nc.tensor.matmul_mx(
-                out=conv[j][:],
+                out=conv[:],
                 lhsT=x_codes[:, pixels].bitcast(FP8X4),
                 lhsT_scale=x_scales[:, pixels],
                 rhs=w_codes[:].bitcast(FP8X4),
@@ -135,9 +136,10 @@ def tile_lvc_pa_s_kernel(tc, x, conv_w, conv_b, codebook, log_smooth, out_0, out
                 start=True,
                 stop=True,
             )
+            return conv
 
-        def add_bias(j):
-            nc.vector.tensor_tensor(out=xp[:, j, :], in0=conv[j][:], in1=bias_rows[:], op=ALU.add)
+        def add_bias(j, conv):
+            nc.vector.tensor_tensor(out=xp[:, j, :], in0=conv[:], in1=bias_rows[:], op=ALU.add)
             nc.sync.dma_start(out=out_0_view[:, j, :], in_=xp[:, j, :])
 
         def sum_squares(j):
@@ -198,15 +200,13 @@ def tile_lvc_pa_s_kernel(tc, x, conv_w, conv_b, codebook, log_smooth, out_0, out
                 stop=True,
             )
 
-        def blocks_of(b):
-            return slice(b * BLOCKS_PER_IMAGE, (b + 1) * BLOCKS_PER_IMAGE)
-
-        def cross_terms(b):
+        def cross_terms(blocks):
+            count = blocks.stop - blocks.start
             nc.vector.scalar_tensor_tensor(
-                out=cross[:, blocks_of(b), :],
-                in0=xc[:, blocks_of(b), :],
+                out=cross[:, blocks, :],
+                in0=xc[:, blocks, :],
                 scalar=-2.0,
-                in1=c2_rows[:].unsqueeze(1).to_broadcast([P, BLOCKS_PER_IMAGE, CODEWORDS]),
+                in1=c2_rows[:].unsqueeze(1).to_broadcast([P, count, CODEWORDS]),
                 op0=ALU.mult,
                 op1=ALU.add,
             )
@@ -221,8 +221,8 @@ def tile_lvc_pa_s_kernel(tc, x, conv_w, conv_b, codebook, log_smooth, out_0, out
                 op1=ALU.mult,
             )
 
-        def find_nearest(j):
-            nc.vector.tensor_reduce(out=nearest[:, j : j + 1], in_=scaled[:, j, :], axis=AXIS.X, op=ALU.min)
+        def find_nearest(blocks):
+            nc.vector.tensor_reduce(out=nearest[:, blocks], in_=scaled[:, blocks, :], axis=AXIS.X, op=ALU.min)
 
         def exponentials(j):
             nc.scalar.activation(
@@ -234,28 +234,35 @@ def tile_lvc_pa_s_kernel(tc, x, conv_w, conv_b, codebook, log_smooth, out_0, out
                 accum_out=weight_sums[:, j : j + 1],
             )
 
-        def invert_sum(j):
-            nc.vector.reciprocal(out=inverse_sums[:, j : j + 1], in_=weight_sums[:, j : j + 1])
+        def invert_sums(blocks):
+            nc.vector.reciprocal(out=inverse_sums[:, blocks], in_=weight_sums[:, blocks])
 
-        def normalise(j):
+        def normalise_on_vector(j):
             nc.vector.tensor_scalar_mul(out=assign[:, j, :], in0=weights[:, j, :], scalar1=inverse_sums[:, j : j + 1])
             nc.sync.dma_start(out=out_1_view[:, j, :], in_=assign[:, j, :])
 
-        nc.sync.dma_start(out=vector_row[:, 0:CHANNELS], in_=conv_b.unsqueeze(0))
-        nc.sync.dma_start(out=vector_row[:, CHANNELS:], in_=log_smooth.unsqueeze(0))
-        nc.vector.memset(ones[:], 1.0)
+        def normalise_on_scalar(j):
+            nc.scalar.activation(
+                out=assign[:, j, :], in_=weights[:, j, :], func=ACT.Copy, scale=inverse_sums[:, j : j + 1]
+            )
+            nc.sync.dma_start(out=out_1_view[:, j, :], in_=assign[:, j, :])
+
         nc.vector.memset(vectors[:], 0.0)
+        nc.vector.memset(ones[:], 1.0)
         load_w(0)
         load_w(1)
+        nc.sync.dma_start(out=vectors[0:1, 0:CHANNELS], in_=conv_b.unsqueeze(0))
+        nc.sync.dma_start(out=vectors[0:1, CHANNELS:], in_=log_smooth.unsqueeze(0))
         load_x(0)
         load_x(1)
         nc.sync.dma_start(out=codebook_raw[:], in_=codebook)
         make_identity(nc, identity_f32[:])
         make_identity(nc, identity_bf16[:])
         nc.scalar.activation(out=table_warmer[:], in_=ones[:, 0:1], func=ACT.Exp)
-
-        nc.vector.tensor_copy(out=vectors[0:1, :], in_=vector_row[:])
-        turn_w(0)
+        w_turned_0 = turn_w(0)
+        w_turned_1 = turn_w(1)
+        w_turned_2 = turn_w(2)
+        w_turned_3 = turn_w(3)
         bias_spread = psum_turned.tile([P, CHANNELS], F32, tag="turned")
         nc.tensor.matmul(out=bias_spread[:], lhsT=ones[:], rhs=vectors[:, 0:CHANNELS], start=True, stop=True)
         small = psum_turned.tile([P, CODEWORDS + PACK], F32, tag="turned")
@@ -269,57 +276,57 @@ def tile_lvc_pa_s_kernel(tc, x, conv_w, conv_b, codebook, log_smooth, out_0, out
                 start=True,
                 stop=True,
             )
-        nc.scalar.activation(out=smooth_rows[:], in_=log_smooth_spread, func=ACT.Exp)
-        nc.scalar.copy(out=bias_columns[:], in_=small[:, CODEWORDS:])
-        regroup_x(nc.vector.tensor_copy, 0, slice(0, PIXELS))
-        nc.vector.tensor_copy(out=bias_rows[:], in_=bias_spread[:])
-        quantise_w(0)
-        quantise_x(0)
-        turn_w(1)
-        regroup_x(nc.scalar.copy, 1, slice(0, P))
-        regroup_x(nc.vector.tensor_copy, 1, slice(P, PIXELS))
-        quantise_w(1)
-        quantise_x(1)
-
-        nc.scalar.activation(
-            out=codebook_squares[:], in_=codebook_raw[:], func=ACT.Square, accum_out=c2_column[:]
-        )
         codebook_turned = psum_turned.tile([P, PACK, CODEWORDS], BF16, tag="turned")
         for t in range(PACK):
             nc.tensor.transpose(
                 out=codebook_turned[:, t, :], in_=codebook_raw[:, t * P : (t + 1) * P], identity=identity_bf16[:]
             )
+        regroup_w(nc.scalar.copy, 0, w_turned_0)
+        regroup_w(nc.scalar.copy, 1, w_turned_1)
+        regroup_w(nc.scalar.copy, 2, w_turned_2)
+        regroup_w(nc.scalar.copy, 3, w_turned_3)
+        regroup_x(nc.vector.tensor_copy, 0, slice(0, PIXELS))
+        quantise_w(0, 2)
+        quantise_x(0)
+        quantise_w(2, 2)
+        nc.scalar.copy(out=bias_rows[:], in_=bias_spread[:])
+        nc.scalar.copy(out=bias_columns[:], in_=small[:, CODEWORDS:])
+        nc.scalar.activation(out=smooth_rows[:], in_=log_smooth_spread, func=ACT.Exp)
+        regroup_x(nc.vector.tensor_copy, 1, slice(0, PIXELS))
+        quantise_x(1)
         nc.scalar.copy(out=codebook_grouped[:], in_=codebook_turned[:].rearrange("p t k -> p k t"))
-
-        convolve(0)
-        convolve(1)
-        convolve(2)
-        conv_turned_3 = convolve_turned(3)
-        convolve(3)
-        add_bias(0)
+        nc.scalar.activation(
+            out=codebook_squares[:], in_=codebook_raw[:], func=ACT.Square, accum_out=c2_column[:]
+        )
+        conv_0 = convolve(0)
+        conv_1 = convolve(1)
+        conv_2 = convolve(2)
+        add_bias(0, conv_0)
         sum_squares(0)
         xp_turned_0 = turn_xp(0)
         regroup_xp(0, xp_turned_0)
-        add_bias(1)
+        add_bias(1, conv_1)
+        conv_turned_3 = convolve_turned(3)
         xp_turned_1 = turn_xp(1)
+        conv_3 = convolve(3)
+        add_bias(2, conv_2)
         regroup_xp(1, xp_turned_1)
-        add_bias(2)
         add_bias_grouped(3, conv_turned_3)
+        c2_turned = psum_turned.tile([P, CODEWORDS], F32, tag="turned")
+        nc.tensor.transpose(out=c2_turned[:], in_=c2_column[:, 0:1].to_broadcast([P, P]), identity=identity_f32[:])
+        xp_turned_2 = turn_xp(2)
+        nc.scalar.copy(out=c2_rows[:], in_=c2_turned[:])
         nc.vector.quantize_mx(
             out=codebook_codes[:].bitcast(FP8X4),
             scales=codebook_scales[:],
             in_=codebook_grouped[:].rearrange("p k t -> p (k t)"),
         )
-        xp_turned_2 = turn_xp(2)
-        c2_turned = psum_turned.tile([P, CODEWORDS], F32, tag="turned")
-        nc.tensor.transpose(out=c2_turned[:], in_=c2_column[:, 0:1].to_broadcast([P, P]), identity=identity_f32[:])
-        regroup_xp(2, xp_turned_2)
-        nc.scalar.copy(out=c2_rows[:], in_=c2_turned[:])
         quantise_xp(0)
         quantise_xp(3)
         multiply_codebook(0)
         multiply_codebook(3)
-        add_bias(3)
+        add_bias(3, conv_3)
+        regroup_xp(2, xp_turned_2)
         quantise_xp(1)
         multiply_codebook(1)
         quantise_xp(2)
@@ -327,26 +334,26 @@ def tile_lvc_pa_s_kernel(tc, x, conv_w, conv_b, codebook, log_smooth, out_0, out
         sum_squares(1)
         sum_squares(2)
         sum_squares(3)
-
-        cross_terms(0)
-        cross_terms(1)
+        cross_terms(slice(0, 1))
+        cross_terms(slice(1, 2))
         scale_distances(0)
         scale_distances(1)
-        find_nearest(0)
-        find_nearest(1)
+        cross_terms(slice(2, 4))
+        find_nearest(slice(0, 1))
+        find_nearest(slice(1, 2))
         exponentials(0)
         exponentials(1)
         scale_distances(2)
         scale_distances(3)
-        find_nearest(2)
-        find_nearest(3)
+        find_nearest(slice(2, 3))
+        find_nearest(slice(3, 4))
         exponentials(2)
         exponentials(3)
-        invert_sum(0)
-        invert_sum(1)
-        normalise(0)
-        normalise(1)
-        invert_sum(2)
-        invert_sum(3)
-        normalise(2)
-        normalise(3)
+        invert_sums(slice(0, 1))
+        invert_sums(slice(1, 2))
+        normalise_on_scalar(0)
+        normalise_on_scalar(1)
+        invert_sums(slice(2, 3))
+        invert_sums(slice(3, 4))
+        normalise_on_scalar(2)
+        normalise_on_vector(3)

@@ -110,18 +110,20 @@ def tile_lvc_pa_s_kernel(tc, x, conv_w, conv_b, codebook, log_smooth, out_0, out
                 out=w_codes[:, words].bitcast(FP8X4), scales=w_scales[:, words], in_=w_grouped[:, values]
             )
 
-        def regroup_x(copy, b, pixels):
+        def regroup_x(copy, first, count):
+            b, start = first // BLOCKS_PER_IMAGE, first % BLOCKS_PER_IMAGE * P
+            pixels = slice(start, start + count * P)
             copy(
                 out=x_grouped[:, b, pixels, :].rearrange("q (c i) t -> q c t i", i=4),
                 in_=x_raw[:, b, :, pixels].rearrange("q t (c i) -> q c t i", i=4),
             )
 
-        def quantise_x(b):
-            words = slice(b * PIXELS, (b + 1) * PIXELS)
+        def quantise_x(first, count):
+            words = slice(first * P, (first + count) * P)
             nc.vector.quantize_mx(
                 out=x_codes[:, words].bitcast(FP8X4),
                 scales=x_scales[:, words],
-                in_=x_grouped[:, b].rearrange("q n t -> q (n t)"),
+                in_=x_grouped[:].rearrange("q b n t -> q (b n t)")[:, first * P * PACK : (first + count) * P * PACK],
             )
 
         def convolve(j):
@@ -155,8 +157,8 @@ def tile_lvc_pa_s_kernel(tc, x, conv_w, conv_b, codebook, log_smooth, out_0, out
                 )
             return xp_turned
 
-        def regroup_xp(j, xp_turned):
-            nc.scalar.copy(out=xp_grouped[:, j], in_=xp_turned[:].rearrange("p t n -> p n t"))
+        def regroup_xp(copy, j, xp_turned):
+            copy(out=xp_grouped[:, j], in_=xp_turned[:].rearrange("p t n -> p n t"))
 
         def convolve_turned(j):
             pixels = slice(j * P, (j + 1) * P)
@@ -285,48 +287,50 @@ def tile_lvc_pa_s_kernel(tc, x, conv_w, conv_b, codebook, log_smooth, out_0, out
         regroup_w(nc.scalar.copy, 1, w_turned_1)
         regroup_w(nc.scalar.copy, 2, w_turned_2)
         regroup_w(nc.scalar.copy, 3, w_turned_3)
-        regroup_x(nc.vector.tensor_copy, 0, slice(0, PIXELS))
-        quantise_w(0, 2)
-        quantise_x(0)
-        quantise_w(2, 2)
+        regroup_x(nc.scalar.copy, 3, 1)
         nc.scalar.copy(out=bias_rows[:], in_=bias_spread[:])
-        nc.scalar.copy(out=bias_columns[:], in_=small[:, CODEWORDS:])
-        nc.scalar.activation(out=smooth_rows[:], in_=log_smooth_spread, func=ACT.Exp)
-        regroup_x(nc.vector.tensor_copy, 1, slice(0, PIXELS))
-        quantise_x(1)
-        nc.scalar.copy(out=codebook_grouped[:], in_=codebook_turned[:].rearrange("p t k -> p k t"))
         nc.scalar.activation(
             out=codebook_squares[:], in_=codebook_raw[:], func=ACT.Square, accum_out=c2_column[:]
         )
+        nc.scalar.copy(out=codebook_grouped[:], in_=codebook_turned[:].rearrange("p t k -> p k t"))
+        regroup_x(nc.vector.tensor_copy, 0, 2)
+        quantise_w(0, 2)
+        quantise_x(0, 2)
+        quantise_w(2, 2)
+        regroup_x(nc.vector.tensor_copy, 2, 1)
+        quantise_x(3, 1)
+        quantise_x(2, 1)
         conv_0 = convolve(0)
         conv_1 = convolve(1)
+        c2_turned = psum_turned.tile([P, CODEWORDS], F32, tag="turned")
+        nc.tensor.transpose(out=c2_turned[:], in_=c2_column[:, 0:1].to_broadcast([P, P]), identity=identity_f32[:])
+        nc.scalar.activation(out=smooth_rows[:], in_=log_smooth_spread, func=ACT.Exp)
+        nc.scalar.copy(out=bias_columns[:], in_=small[:, CODEWORDS:])
+        nc.scalar.copy(out=c2_rows[:], in_=c2_turned[:])
         conv_2 = convolve(2)
         add_bias(0, conv_0)
         sum_squares(0)
         xp_turned_0 = turn_xp(0)
-        regroup_xp(0, xp_turned_0)
+        regroup_xp(nc.scalar.copy, 0, xp_turned_0)
         add_bias(1, conv_1)
         conv_turned_3 = convolve_turned(3)
         xp_turned_1 = turn_xp(1)
-        conv_3 = convolve(3)
-        add_bias(2, conv_2)
-        regroup_xp(1, xp_turned_1)
-        add_bias_grouped(3, conv_turned_3)
-        c2_turned = psum_turned.tile([P, CODEWORDS], F32, tag="turned")
-        nc.tensor.transpose(out=c2_turned[:], in_=c2_column[:, 0:1].to_broadcast([P, P]), identity=identity_f32[:])
-        xp_turned_2 = turn_xp(2)
-        nc.scalar.copy(out=c2_rows[:], in_=c2_turned[:])
         nc.vector.quantize_mx(
             out=codebook_codes[:].bitcast(FP8X4),
             scales=codebook_scales[:],
             in_=codebook_grouped[:].rearrange("p k t -> p (k t)"),
         )
+        conv_3 = convolve(3)
+        add_bias(2, conv_2)
+        regroup_xp(nc.scalar.copy, 1, xp_turned_1)
+        add_bias_grouped(3, conv_turned_3)
+        xp_turned_2 = turn_xp(2)
         quantise_xp(0)
         quantise_xp(3)
         multiply_codebook(0)
         multiply_codebook(3)
         add_bias(3, conv_3)
-        regroup_xp(2, xp_turned_2)
+        regroup_xp(nc.scalar.copy, 2, xp_turned_2)
         quantise_xp(1)
         multiply_codebook(1)
         quantise_xp(2)

@@ -39,11 +39,12 @@ def tile_lvc_pa_s_kernel(tc, x, conv_w, conv_b, codebook, log_smooth, out_0, out
         table_warmer = keep.tile([P, 1], F32)
         identity_f32 = keep.tile([P, P], F32)
         identity_bf16 = keep.tile([P, P], BF16)
-        bias_rows = keep.tile([P, CHANNELS], F32)
-        bias_columns = keep.tile([P, PACK], F32)
+        bias_rows = keep.tile([P, CHANNELS], BF16)
         smooth_rows = keep.tile([P, CODEWORDS], F32)
         c2_column = keep.tile([P, 1], F32)
-        c2_rows = keep.tile([P, CODEWORDS], F32)
+        late_constants = keep.tile([P, CODEWORDS + PACK], F32)
+        c2_rows = late_constants[:, 0:CODEWORDS]
+        bias_columns = late_constants[:, CODEWORDS:]
 
         w_raw = keep.tile([P, CHANNEL_BLOCKS, CHANNELS], BF16)
         w_grouped = keep.tile([P, CHANNELS * PACK], BF16, align_bytes=64)
@@ -180,7 +181,7 @@ def tile_lvc_pa_s_kernel(tc, x, conv_w, conv_b, codebook, log_smooth, out_0, out
             nc.vector.tensor_tensor(
                 out=xp_grouped[:, j],
                 in0=conv_turned[:].rearrange("p t n -> p n t"),
-                in1=bias_columns[:].unsqueeze(1).to_broadcast([P, P, PACK]),
+                in1=bias_columns.unsqueeze(1).to_broadcast([P, P, PACK]),
                 op=ALU.add,
             )
 
@@ -208,7 +209,7 @@ def tile_lvc_pa_s_kernel(tc, x, conv_w, conv_b, codebook, log_smooth, out_0, out
                 out=cross[:, blocks, :],
                 in0=xc[:, blocks, :],
                 scalar=-2.0,
-                in1=c2_rows[:].unsqueeze(1).to_broadcast([P, count, CODEWORDS]),
+                in1=c2_rows.unsqueeze(1).to_broadcast([P, count, CODEWORDS]),
                 op0=ALU.mult,
                 op1=ALU.add,
             )
@@ -265,19 +266,10 @@ def tile_lvc_pa_s_kernel(tc, x, conv_w, conv_b, codebook, log_smooth, out_0, out
         w_turned_1 = turn_w(1)
         w_turned_2 = turn_w(2)
         w_turned_3 = turn_w(3)
-        bias_spread = psum_turned.tile([P, CHANNELS], F32, tag="turned")
+        bias_spread = psum_turned.tile([P, CHANNELS], BF16, tag="turned")
         nc.tensor.matmul(out=bias_spread[:], lhsT=ones[:], rhs=vectors[:, 0:CHANNELS], start=True, stop=True)
-        small = psum_turned.tile([P, CODEWORDS + PACK], F32, tag="turned")
-        log_smooth_spread = small[:, 0:CODEWORDS]
-        nc.tensor.matmul(out=log_smooth_spread, lhsT=ones[:], rhs=vectors[:, CHANNELS:], start=True, stop=True)
-        for t in range(PACK):
-            nc.tensor.matmul(
-                out=small[:, CODEWORDS + t : CODEWORDS + t + 1],
-                lhsT=vectors[:, t * P : (t + 1) * P],
-                rhs=ones[:, 0:1],
-                start=True,
-                stop=True,
-            )
+        log_smooth_spread = psum_turned.tile([P, CODEWORDS], F32, tag="turned")
+        nc.tensor.matmul(out=log_smooth_spread[:], lhsT=ones[:], rhs=vectors[:, CHANNELS:], start=True, stop=True)
         codebook_turned = psum_turned.tile([P, PACK, CODEWORDS], BF16, tag="turned")
         for t in range(PACK):
             nc.tensor.transpose(
@@ -298,15 +290,23 @@ def tile_lvc_pa_s_kernel(tc, x, conv_w, conv_b, codebook, log_smooth, out_0, out
         quantise_x(0, 2)
         quantise_w(2, 2)
         regroup_x(nc.vector.tensor_copy, 2, 1)
-        quantise_x(3, 1)
-        quantise_x(2, 1)
+        quantise_x(2, 2)
         conv_0 = convolve(0)
         conv_1 = convolve(1)
-        c2_turned = psum_turned.tile([P, CODEWORDS], F32, tag="turned")
-        nc.tensor.transpose(out=c2_turned[:], in_=c2_column[:, 0:1].to_broadcast([P, P]), identity=identity_f32[:])
-        nc.scalar.activation(out=smooth_rows[:], in_=log_smooth_spread, func=ACT.Exp)
-        nc.scalar.copy(out=bias_columns[:], in_=small[:, CODEWORDS:])
-        nc.scalar.copy(out=c2_rows[:], in_=c2_turned[:])
+        late_spread = psum_turned.tile([P, CODEWORDS + PACK], F32, tag="turned")
+        nc.tensor.transpose(
+            out=late_spread[:, 0:CODEWORDS], in_=c2_column[:, 0:1].to_broadcast([P, P]), identity=identity_f32[:]
+        )
+        for t in range(PACK):
+            nc.tensor.matmul(
+                out=late_spread[:, CODEWORDS + t : CODEWORDS + t + 1],
+                lhsT=vectors[:, t * P : (t + 1) * P],
+                rhs=ones[:, 0:1],
+                start=True,
+                stop=True,
+            )
+        nc.scalar.activation(out=smooth_rows[:], in_=log_smooth_spread[:], func=ACT.Exp)
+        nc.scalar.copy(out=late_constants[:], in_=late_spread[:])
         conv_2 = convolve(2)
         add_bias(0, conv_0)
         sum_squares(0)

@@ -63,9 +63,10 @@ def tile_lvc_pa_s_kernel(tc, x, conv_w, conv_b, codebook, log_smooth, out_0, out
         xp = keep.tile([P, PIXEL_BLOCKS, CHANNELS], F32)
         xp_squares = keep.tile([P, PIXEL_BLOCKS, CHANNELS], BF16)
         x2 = keep.tile([P, PIXEL_BLOCKS], F32)
+        slot = {0: 0, 3: 1, 1: 2, 2: 3}
         xp_grouped = keep.tile([P, PIXEL_BLOCKS, P, PACK], BF16, align_bytes=64)
-        xp_codes = keep.tile([P, PIXEL_BLOCKS, P], U32, align_bytes=64)
-        xp_scales = keep.tile([P, PIXEL_BLOCKS, P], U8, align_bytes=64)
+        xp_codes = keep.tile([P, PIXEL_BLOCKS * P], U32, align_bytes=64)
+        xp_scales = keep.tile([P, PIXEL_BLOCKS * P], U8, align_bytes=64)
         xc = psum_xc.tile([P, PIXEL_BLOCKS, CODEWORDS], F32)
         cross = keep.tile([P, PIXEL_BLOCKS, CODEWORDS], F32)
         scaled = keep.tile([P, PIXEL_BLOCKS, CODEWORDS], F32)
@@ -159,7 +160,7 @@ def tile_lvc_pa_s_kernel(tc, x, conv_w, conv_b, codebook, log_smooth, out_0, out
             return xp_turned
 
         def regroup_xp(copy, j, xp_turned):
-            copy(out=xp_grouped[:, j], in_=xp_turned[:].rearrange("p t n -> p n t"))
+            copy(out=xp_grouped[:, slot[j]], in_=xp_turned[:].rearrange("p t n -> p n t"))
 
         def convolve_turned(j):
             pixels = slice(j * P, (j + 1) * P)
@@ -179,24 +180,27 @@ def tile_lvc_pa_s_kernel(tc, x, conv_w, conv_b, codebook, log_smooth, out_0, out
 
         def add_bias_grouped(j, conv_turned):
             nc.vector.tensor_tensor(
-                out=xp_grouped[:, j],
+                out=xp_grouped[:, slot[j]],
                 in0=conv_turned[:].rearrange("p t n -> p n t"),
                 in1=bias_columns.unsqueeze(1).to_broadcast([P, P, PACK]),
                 op=ALU.add,
             )
 
-        def quantise_xp(j):
+        def quantise_xp(first, count):
+            words = slice(slot[first] * P, (slot[first] + count) * P)
+            values = slice(slot[first] * P * PACK, (slot[first] + count) * P * PACK)
             nc.vector.quantize_mx(
-                out=xp_codes[:, j, :].bitcast(FP8X4),
-                scales=xp_scales[:, j, :],
-                in_=xp_grouped[:, j].rearrange("p n t -> p (n t)"),
+                out=xp_codes[:, words].bitcast(FP8X4),
+                scales=xp_scales[:, words],
+                in_=xp_grouped[:].rearrange("p s n t -> p (s n t)")[:, values],
             )
 
         def multiply_codebook(j):
+            words = slice(slot[j] * P, (slot[j] + 1) * P)
             nc.tensor.matmul_mx(
                 out=xc[:, j, :],
-                lhsT=xp_codes[:, j, :].bitcast(FP8X4),
-                lhsT_scale=xp_scales[:, j, :],
+                lhsT=xp_codes[:, words].bitcast(FP8X4),
+                lhsT_scale=xp_scales[:, words],
                 rhs=codebook_codes[:].bitcast(FP8X4),
                 rhs_scale=codebook_scales[:],
                 start=True,
@@ -325,15 +329,14 @@ def tile_lvc_pa_s_kernel(tc, x, conv_w, conv_b, codebook, log_smooth, out_0, out
         regroup_xp(nc.scalar.copy, 1, xp_turned_1)
         add_bias_grouped(3, conv_turned_3)
         xp_turned_2 = turn_xp(2)
-        quantise_xp(0)
-        quantise_xp(3)
+        quantise_xp(0, 2)
         multiply_codebook(0)
         multiply_codebook(3)
         add_bias(3, conv_3)
         regroup_xp(nc.scalar.copy, 2, xp_turned_2)
-        quantise_xp(1)
+        quantise_xp(1, 1)
         multiply_codebook(1)
-        quantise_xp(2)
+        quantise_xp(2, 1)
         multiply_codebook(2)
         sum_squares(1)
         sum_squares(2)
@@ -343,8 +346,7 @@ def tile_lvc_pa_s_kernel(tc, x, conv_w, conv_b, codebook, log_smooth, out_0, out
         scale_distances(0)
         scale_distances(1)
         cross_terms(slice(2, 4))
-        find_nearest(slice(0, 1))
-        find_nearest(slice(1, 2))
+        find_nearest(slice(0, 2))
         exponentials(0)
         exponentials(1)
         scale_distances(2)
@@ -353,11 +355,9 @@ def tile_lvc_pa_s_kernel(tc, x, conv_w, conv_b, codebook, log_smooth, out_0, out
         find_nearest(slice(3, 4))
         exponentials(2)
         exponentials(3)
-        invert_sums(slice(0, 1))
-        invert_sums(slice(1, 2))
+        invert_sums(slice(0, 2))
         normalise_on_scalar(0)
         normalise_on_scalar(1)
-        invert_sums(slice(2, 3))
-        invert_sums(slice(3, 4))
+        invert_sums(slice(2, 4))
         normalise_on_scalar(2)
         normalise_on_vector(3)

@@ -67,7 +67,6 @@ def tile_lvc_pa_s_kernel(tc, x, conv_w, conv_b, codebook, log_smooth, out_0, out
         xp_grouped = keep.tile([P, PIXEL_BLOCKS, P, PACK], BF16, align_bytes=64)
         xp_codes = keep.tile([P, PIXEL_BLOCKS * P], U32, align_bytes=64)
         xp_scales = keep.tile([P, PIXEL_BLOCKS * P], U8, align_bytes=64)
-        xc = psum_xc.tile([P, PIXEL_BLOCKS, CODEWORDS], F32)
         cross = keep.tile([P, PIXEL_BLOCKS, CODEWORDS], F32)
         scaled = keep.tile([P, PIXEL_BLOCKS, CODEWORDS], F32)
         nearest = keep.tile([P, PIXEL_BLOCKS], F32)
@@ -195,10 +194,10 @@ def tile_lvc_pa_s_kernel(tc, x, conv_w, conv_b, codebook, log_smooth, out_0, out
                 in_=xp_grouped[:].rearrange("p s n t -> p (s n t)")[:, values],
             )
 
-        def multiply_codebook(j):
+        def multiply_codebook(j, product):
             words = slice(slot[j] * P, (slot[j] + 1) * P)
             nc.tensor.matmul_mx(
-                out=xc[:, j, :],
+                out=product,
                 lhsT=xp_codes[:, words].bitcast(FP8X4),
                 lhsT_scale=xp_scales[:, words],
                 rhs=codebook_codes[:].bitcast(FP8X4),
@@ -207,11 +206,11 @@ def tile_lvc_pa_s_kernel(tc, x, conv_w, conv_b, codebook, log_smooth, out_0, out
                 stop=True,
             )
 
-        def cross_terms(blocks):
-            count = blocks.stop - blocks.start
+        def cross_terms(first, xc):
+            count = xc.shape[1]
             nc.vector.scalar_tensor_tensor(
-                out=cross[:, blocks, :],
-                in0=xc[:, blocks, :],
+                out=cross[:, first : first + count, :],
+                in0=xc[:],
                 scalar=-2.0,
                 in1=c2_rows.unsqueeze(1).to_broadcast([P, count, CODEWORDS]),
                 op0=ALU.mult,
@@ -319,33 +318,36 @@ def tile_lvc_pa_s_kernel(tc, x, conv_w, conv_b, codebook, log_smooth, out_0, out
         add_bias(1, conv_1)
         conv_turned_3 = convolve_turned(3)
         xp_turned_1 = turn_xp(1)
+        conv_3 = convolve(3)
+        add_bias(2, conv_2)
+        regroup_xp(nc.scalar.copy, 1, xp_turned_1)
+        add_bias_grouped(3, conv_turned_3)
         nc.vector.quantize_mx(
             out=codebook_codes[:].bitcast(FP8X4),
             scales=codebook_scales[:],
             in_=codebook_grouped[:].rearrange("p k t -> p (k t)"),
         )
-        conv_3 = convolve(3)
-        add_bias(2, conv_2)
-        regroup_xp(nc.scalar.copy, 1, xp_turned_1)
-        add_bias_grouped(3, conv_turned_3)
         xp_turned_2 = turn_xp(2)
         quantise_xp(0, 2)
-        multiply_codebook(0)
-        multiply_codebook(3)
+        xc_0 = psum_conv.tile([P, 1, CODEWORDS], F32, name="xc", tag="conv")
+        xc_1 = psum_conv.tile([P, 1, CODEWORDS], F32, name="xc", tag="conv")
+        xc_23 = psum_xc.tile([P, 2, CODEWORDS], F32)
+        multiply_codebook(0, xc_0[:, 0, :])
+        multiply_codebook(3, xc_23[:, 1, :])
         add_bias(3, conv_3)
         regroup_xp(nc.scalar.copy, 2, xp_turned_2)
         quantise_xp(1, 1)
-        multiply_codebook(1)
+        multiply_codebook(1, xc_1[:, 0, :])
         quantise_xp(2, 1)
-        multiply_codebook(2)
+        multiply_codebook(2, xc_23[:, 0, :])
         sum_squares(1)
         sum_squares(2)
         sum_squares(3)
-        cross_terms(slice(0, 1))
-        cross_terms(slice(1, 2))
+        cross_terms(0, xc_0)
+        cross_terms(1, xc_1)
         scale_distances(0)
         scale_distances(1)
-        cross_terms(slice(2, 4))
+        cross_terms(2, xc_23)
         find_nearest(slice(0, 2))
         exponentials(0)
         exponentials(1)
@@ -356,8 +358,8 @@ def tile_lvc_pa_s_kernel(tc, x, conv_w, conv_b, codebook, log_smooth, out_0, out
         exponentials(2)
         exponentials(3)
         invert_sums(slice(0, 2))
-        normalise_on_scalar(0)
+        normalise_on_vector(0)
         normalise_on_scalar(1)
         invert_sums(slice(2, 4))
-        normalise_on_scalar(2)
         normalise_on_vector(3)
+        normalise_on_scalar(2)

from contextlib import ExitStack

import concourse.mybir as mybir
from concourse.masks import make_identity

F32 = mybir.dt.float32
BF16 = mybir.dt.bfloat16
U32 = mybir.dt.uint32
U8 = mybir.dt.uint8
FP8X4 = mybir.dt.float8_e4m3fn_x4
ALU = mybir.AluOpType
ACT = mybir.ActivationFunctionType
AXIS = mybir.AxisListType

P = 128
PACK = 4
IMAGES = 2
CHANNELS = 512
PIXELS = 256
CODEWORDS = 128
BLOCKS_PER_IMAGE = PIXELS // P
PIXEL_BLOCKS = IMAGES * BLOCKS_PER_IMAGE
CHANNEL_BLOCKS = CHANNELS // P

FLOPS = 2 * IMAGES * PIXELS * CHANNELS * (CHANNELS + CODEWORDS)


def tile_lvc_pa_s_kernel(tc, x, conv_w, conv_b, codebook, log_smooth, out_0, out_1):
    nc = tc.nc
    with ExitStack() as ctx:
        keep = ctx.enter_context(tc.tile_pool(name="keep", bufs=1))
        psum_turned = ctx.enter_context(tc.psum_pool(name="psum_turned", bufs=3))
        psum_conv = ctx.enter_context(tc.psum_pool(name="psum_conv", bufs=PIXEL_BLOCKS))
        psum_xc = ctx.enter_context(tc.psum_pool(name="psum_xc", bufs=1))
        ctx.enter_context(tc.manual_schedule())

        vectors = keep.tile([P, CHANNELS + CODEWORDS], BF16)
        ones = keep.tile([P, P], BF16)
        table_warmer = keep.tile([P, 1], F32)
        identity_f32 = keep.tile([P, P], F32)
        identity_bf16 = keep.tile([P, P], BF16)
        bias_rows = keep.tile([P, CHANNELS], BF16)
        smooth_rows = keep.tile([P, CODEWORDS], F32)
        c2_column = keep.tile([P, 1], F32)
        late_constants = keep.tile([P, CODEWORDS + PACK], F32)
        c2_rows = late_constants[:, 0:CODEWORDS]
        bias_columns = late_constants[:, CODEWORDS:]

        w_raw = keep.tile([P, CHANNEL_BLOCKS, CHANNELS], BF16)
        w_grouped = keep.tile([P, CHANNELS * PACK], BF16, align_bytes=64)
        w_codes = keep.tile([P, CHANNELS], U32, align_bytes=64)
        w_scales = keep.tile([P, CHANNELS], U8, align_bytes=64)
        x_raw = keep.tile([P, IMAGES, PACK, PIXELS], BF16)
        x_grouped = keep.tile([P, IMAGES, PIXELS, PACK], BF16, align_bytes=64)
        x_codes = keep.tile([P, IMAGES * PIXELS], U32, align_bytes=64)
        x_scales = keep.tile([P, IMAGES * PIXELS], U8, align_bytes=64)
        codebook_raw = keep.tile([P, CHANNELS], BF16)
        codebook_squares = keep.tile([P, CHANNELS], BF16)
        codebook_grouped = keep.tile([P, CODEWORDS, PACK], BF16, align_bytes=64)
        codebook_codes = keep.tile([P, CODEWORDS], U32, align_bytes=64)
        codebook_scales = keep.tile([P, CODEWORDS], U8, align_bytes=64)

        xp = keep.tile([P, PIXEL_BLOCKS, CHANNELS], F32)
        xp_squares = keep.tile([P, PIXEL_BLOCKS, CHANNELS], BF16)
        x2 = keep.tile([P, PIXEL_BLOCKS], F32)
        slot = {0: 0, 3: 1, 1: 2, 2: 3}
        xp_grouped = keep.tile([P, PIXEL_BLOCKS, P, PACK], BF16, align_bytes=64)
        xp_codes = keep.tile([P, PIXEL_BLOCKS * P], U32, align_bytes=64)
        xp_scales = keep.tile([P, PIXEL_BLOCKS * P], U8, align_bytes=64)
        cross = keep.tile([P, PIXEL_BLOCKS, CODEWORDS], F32)
        scaled = keep.tile([P, PIXEL_BLOCKS, CODEWORDS], F32)
        nearest = keep.tile([P, PIXEL_BLOCKS], F32)
        weights = keep.tile([P, PIXEL_BLOCKS, CODEWORDS], F32)
        weight_sums = keep.tile([P, PIXEL_BLOCKS], F32)
        inverse_sums = keep.tile([P, PIXEL_BLOCKS], F32)
        assign = keep.tile([P, PIXEL_BLOCKS, CODEWORDS], F32)
        out_0_view = out_0.rearrange("b (s p) c -> p (b s) c", p=P)
        out_1_view = out_1.rearrange("b (s p) k -> p (b s) k", p=P)

        def load_w(half):
            obs = slice(2 * half, 2 * half + 2)
            nc.sync.dma_start(out=w_raw[:, obs, :], in_=conv_w.rearrange("(ob p) c -> p ob c", p=P)[:, obs, :])

        def load_x(b):
            nc.sync.dma_start(
                out=x_raw[:, b].rearrange("q (u e) n -> q u (e n)", u=2),
                in_=x[b].rearrange("(u q e) h w -> q u (e h w)", u=2, e=2),
            )

        def turn_w(ob):
            w_turned = psum_conv.tile([P, 2, P], F32, name="w_turned", tag="conv")
            for u in range(2):
                nc.tensor.transpose(
                    out=w_turned[:, u, :],
                    in_=w_raw[:, ob, 2 * P * u : 2 * P * (u + 1)].bitcast(F32),
                    identity=identity_f32[:],
                )
            return w_turned

        def regroup_w(copy, ob, w_turned):
            values = slice(ob * P * PACK, (ob + 1) * P * PACK)
            copy(
                out=w_grouped[:, values].bitcast(F32).rearrange("p (o u) -> p o u", u=2),
                in_=w_turned[:].rearrange("p u o -> p o u"),
            )

        def quantise_w(first, count):
            values = slice(first * P * PACK, (first + count) * P * PACK)
            words = slice(first * P, (first + count) * P)
            nc.vector.quantize_mx(
                out=w_codes[:, words].bitcast(FP8X4), scales=w_scales[:, words], in_=w_grouped[:, values]
            )

        def regroup_x(copy, first, count):
            b, start = first // BLOCKS_PER_IMAGE, first % BLOCKS_PER_IMAGE * P
            pixels = slice(start, start + count * P)
            copy(
                out=x_grouped[:, b, pixels, :].rearrange("q (c i) t -> q c t i", i=4),
                in_=x_raw[:, b, :, pixels].rearrange("q t (c i) -> q c t i", i=4),
            )

        def quantise_x(first, count):
            words = slice(first * P, (first + count) * P)
            nc.vector.quantize_mx(
                out=x_codes[:, words].bitcast(FP8X4),
                scales=x_scales[:, words],
                in_=x_grouped[:].rearrange("q b n t -> q (b n t)")[:, first * P * PACK : (first + count) * P * PACK],
            )

        def convolve(j):
            pixels = slice(j * P, (j + 1) * P)
            conv = psum_conv.tile([P, CHANNELS], F32, name="conv", tag="conv")
            nc.tensor.matmul_mx(
                out=conv[:],
                lhsT=x_codes[:, pixels].bitcast(FP8X4),
                lhsT_scale=x_scales[:, pixels],
                rhs=w_codes[:].bitcast(FP8X4),
                rhs_scale=w_scales[:],
                start=True,
                stop=True,
            )
            return conv

        def add_bias(j, conv):
            nc.vector.tensor_tensor(out=xp[:, j, :], in0=conv[:], in1=bias_rows[:], op=ALU.add)
            nc.sync.dma_start(out=out_0_view[:, j, :], in_=xp[:, j, :])

        def sum_squares(j):
            nc.scalar.activation(
                out=xp_squares[:, j, :], in_=xp[:, j, :], func=ACT.Square, accum_out=x2[:, j : j + 1]
            )

        def turn_xp(j):
            xp_turned = psum_turned.tile([P, PACK, P], F32, tag="turned")
            for t in range(PACK):
                nc.tensor.transpose(
                    out=xp_turned[:, t, :], in_=xp[:, j, t * P : (t + 1) * P], identity=identity_f32[:]
                )
            return xp_turned

        def regroup_xp(copy, j, xp_turned):
            copy(out=xp_grouped[:, slot[j]], in_=xp_turned[:].rearrange("p t n -> p n t"))

        def convolve_turned(j):
            pixels = slice(j * P, (j + 1) * P)
            conv_turned = psum_turned.tile([P, PACK, P], F32, tag="turned")
            for t in range(PACK):
                channels = slice(t * P, (t + 1) * P)
                nc.tensor.matmul_mx(
                    out=conv_turned[:, t, :],
                    lhsT=w_codes[:, channels].bitcast(FP8X4),
                    lhsT_scale=w_scales[:, channels],
                    rhs=x_codes[:, pixels].bitcast(FP8X4),
                    rhs_scale=x_scales[:, pixels],
                    start=True,
                    stop=True,
                )
            return conv_turned

        def add_bias_grouped(j, conv_turned):
            nc.vector.tensor_tensor(
                out=xp_grouped[:, slot[j]],
                in0=conv_turned[:].rearrange("p t n -> p n t"),
                in1=bias_columns.unsqueeze(1).to_broadcast([P, P, PACK]),
                op=ALU.add,
            )

        def quantise_xp(first, count):
            words = slice(slot[first] * P, (slot[first] + count) * P)
            values = slice(slot[first] * P * PACK, (slot[first] + count) * P * PACK)
            nc.vector.quantize_mx(
                out=xp_codes[:, words].bitcast(FP8X4),
                scales=xp_scales[:, words],
                in_=xp_grouped[:].rearrange("p s n t -> p (s n t)")[:, values],
            )

        def multiply_codebook(j, product):
            words = slice(slot[j] * P, (slot[j] + 1) * P)
            nc.tensor.matmul_mx(
                out=product,
                lhsT=xp_codes[:, words].bitcast(FP8X4),
                lhsT_scale=xp_scales[:, words],
                rhs=codebook_codes[:].bitcast(FP8X4),
                rhs_scale=codebook_scales[:],
                start=True,
                stop=True,
            )

        def cross_terms(first, xc):
            count = xc.shape[1]
            nc.vector.scalar_tensor_tensor(
                out=cross[:, first : first + count, :],
                in0=xc[:],
                scalar=-2.0,
                in1=c2_rows.unsqueeze(1).to_broadcast([P, count, CODEWORDS]),
                op0=ALU.mult,
                op1=ALU.add,
            )

        def scale_distances(j):
            nc.vector.scalar_tensor_tensor(
                out=scaled[:, j, :],
                in0=cross[:, j, :],
                scalar=x2[:, j : j + 1],
                in1=smooth_rows[:],
                op0=ALU.add,
                op1=ALU.mult,
            )

        def find_nearest(blocks):
            nc.vector.tensor_reduce(out=nearest[:, blocks], in_=scaled[:, blocks, :], axis=AXIS.X, op=ALU.min)

        def exponentials(j):
            nc.scalar.activation(
                out=weights[:, j, :],
                in_=scaled[:, j, :],
                func=ACT.Exp,
                scale=-1.0,
                bias=nearest[:, j : j + 1],
                accum_out=weight_sums[:, j : j + 1],
            )

        def invert_sums(blocks):
            nc.vector.reciprocal(out=inverse_sums[:, blocks], in_=weight_sums[:, blocks])

        def normalise_on_vector(j):
            nc.vector.tensor_scalar_mul(out=assign[:, j, :], in0=weights[:, j, :], scalar1=inverse_sums[:, j : j + 1])
            nc.sync.dma_start(out=out_1_view[:, j, :], in_=assign[:, j, :])

        def normalise_on_scalar(j):
            nc.scalar.activation(
                out=assign[:, j, :], in_=weights[:, j, :], func=ACT.Copy, scale=inverse_sums[:, j : j + 1]
            )
            nc.sync.dma_start(out=out_1_view[:, j, :], in_=assign[:, j, :])

        nc.vector.memset(vectors[:], 0.0)
        nc.vector.memset(ones[:], 1.0)
        load_w(0)
        load_w(1)
        nc.sync.dma_start(out=vectors[0:1, 0:CHANNELS], in_=conv_b.unsqueeze(0))
        nc.sync.dma_start(out=vectors[0:1, CHANNELS:], in_=log_smooth.unsqueeze(0))
        load_x(0)
        load_x(1)
        nc.sync.dma_start(out=codebook_raw[:], in_=codebook)
        make_identity(nc, identity_f32[:])
        make_identity(nc, identity_bf16[:])
        nc.scalar.activation(out=table_warmer[:], in_=ones[:, 0:1], func=ACT.Exp)
        w_turned_0 = turn_w(0)
        w_turned_1 = turn_w(1)
        w_turned_2 = turn_w(2)
        w_turned_3 = turn_w(3)
        bias_spread = psum_turned.tile([P, CHANNELS], BF16, tag="turned")
        nc.tensor.matmul(out=bias_spread[:], lhsT=ones[:], rhs=vectors[:, 0:CHANNELS], start=True, stop=True)
        log_smooth_spread = psum_turned.tile([P, CODEWORDS], F32, tag="turned")
        nc.tensor.matmul(out=log_smooth_spread[:], lhsT=ones[:], rhs=vectors[:, CHANNELS:], start=True, stop=True)
        codebook_turned = psum_turned.tile([P, PACK, CODEWORDS], BF16, tag="turned")
        for t in range(PACK):
            nc.tensor.transpose(
                out=codebook_turned[:, t, :], in_=codebook_raw[:, t * P : (t + 1) * P], identity=identity_bf16[:]
            )
        regroup_w(nc.scalar.copy, 0, w_turned_0)
        regroup_w(nc.scalar.copy, 1, w_turned_1)
        regroup_w(nc.scalar.copy, 2, w_turned_2)
        regroup_w(nc.scalar.copy, 3, w_turned_3)
        regroup_x(nc.scalar.copy, 3, 1)
        nc.scalar.copy(out=bias_rows[:], in_=bias_spread[:])
        nc.scalar.activation(
            out=codebook_squares[:], in_=codebook_raw[:], func=ACT.Square, accum_out=c2_column[:]
        )
        nc.scalar.copy(out=codebook_grouped[:], in_=codebook_turned[:].rearrange("p t k -> p k t"))
        regroup_x(nc.vector.tensor_copy, 0, 2)
        quantise_w(0, 2)
        quantise_x(0, 2)
        quantise_w(2, 2)
        regroup_x(nc.vector.tensor_copy, 2, 1)
        quantise_x(2, 2)
        conv_0 = convolve(0)
        conv_1 = convolve(1)
        late_spread = psum_turned.tile([P, CODEWORDS + PACK], F32, tag="turned")
        nc.tensor.transpose(
            out=late_spread[:, 0:CODEWORDS], in_=c2_column[:, 0:1].to_broadcast([P, P]), identity=identity_f32[:]
        )
        for t in range(PACK):
            nc.tensor.matmul(
                out=late_spread[:, CODEWORDS + t : CODEWORDS + t + 1],
                lhsT=vectors[:, t * P : (t + 1) * P],
                rhs=ones[:, 0:1],
                start=True,
                stop=True,
            )
        nc.scalar.activation(out=smooth_rows[:], in_=log_smooth_spread[:], func=ACT.Exp)
        nc.scalar.copy(out=late_constants[:], in_=late_spread[:])
        conv_2 = convolve(2)
        add_bias(0, conv_0)
        sum_squares(0)
        xp_turned_0 = turn_xp(0)
        regroup_xp(nc.scalar.copy, 0, xp_turned_0)
        add_bias(1, conv_1)
        conv_turned_3 = convolve_turned(3)
        xp_turned_1 = turn_xp(1)
        conv_3 = convolve(3)
        add_bias(2, conv_2)
        regroup_xp(nc.scalar.copy, 1, xp_turned_1)
        add_bias_grouped(3, conv_turned_3)
        nc.vector.quantize_mx(
            out=codebook_codes[:].bitcast(FP8X4),
            scales=codebook_scales[:],
            in_=codebook_grouped[:].rearrange("p k t -> p (k t)"),
        )
        xp_turned_2 = turn_xp(2)
        quantise_xp(0, 2)
        xc_0 = psum_conv.tile([P, 1, CODEWORDS], F32, name="xc", tag="conv")
        xc_1 = psum_conv.tile([P, 1, CODEWORDS], F32, name="xc", tag="conv")
        xc_23 = psum_xc.tile([P, 2, CODEWORDS], F32)
        multiply_codebook(0, xc_0[:, 0, :])
        multiply_codebook(3, xc_23[:, 1, :])
        add_bias(3, conv_3)
        regroup_xp(nc.scalar.copy, 2, xp_turned_2)
        quantise_xp(1, 1)
        multiply_codebook(1, xc_1[:, 0, :])
        quantise_xp(2, 1)
        multiply_codebook(2, xc_23[:, 0, :])
        sum_squares(1)
        sum_squares(2)
        sum_squares(3)
        cross_terms(0, xc_0)
        cross_terms(1, xc_1)
        scale_distances(0)
        scale_distances(1)
        cross_terms(2, xc_23)
        find_nearest(slice(0, 2))
        exponentials(0)
        exponentials(1)
        scale_distances(2)
        scale_distances(3)
        find_nearest(slice(2, 3))
        find_nearest(slice(3, 4))
        exponentials(2)
        exponentials(3)
        invert_sums(slice(0, 2))
        normalise_on_vector(0)
        normalise_on_scalar(1)
        invert_sums(slice(2, 4))
        normalise_on_vector(3)
        normalise_on_scalar(2)
